import numpy as np
import ml_dtypes


def mxq(x, axis, fmt="e4m3"):
    dtype, down = {"e4m3": (ml_dtypes.float8_e4m3fn, 7), "e5m2": (ml_dtypes.float8_e5m2, 14)}[fmt]
    v = np.moveaxis(np.asarray(x, np.float32).astype(ml_dtypes.bfloat16).astype(np.float64), axis, -1)
    blocks = v.reshape(v.shape[:-1] + (-1, 32))
    amax = np.abs(blocks).max(-1, keepdims=True)
    byte = np.maximum(np.where(amax > 0, np.frexp(amax)[1] - 1 + 127, 0) - down, 1)
    scale = np.exp2(byte - 127.0)
    codes = (blocks / scale).astype(np.float32).astype(dtype).astype(np.float64)
    return np.moveaxis((codes * scale).reshape(v.shape), -1, axis)


WIDE = False


def mx_kscale(k):
    if not WIDE:
        return np.ones(k)
    levels = np.array([10, -10, 5, -5, 0])
    a = np.random.permutation(np.resize(levels, k // 512 * 4)).reshape(k // 512, 4)
    idx = np.arange(k)
    return np.exp2(a[idx // 512, idx % 128 // 32])


BF16 = ml_dtypes.bfloat16


def bf(x):
    return np.asarray(x, np.float32).astype(BF16)


def f64(x):
    return np.asarray(x).astype(np.float64)


B, S, V, E, M = 512, 16, 4096, 512, 1024


def setup_inputs():
    s, t = mx_kscale(E), mx_kscale(M)
    return {"y2": bf(np.maximum(np.random.standard_normal((B, E)), 0.0) * s),
            "first": bf(np.random.standard_normal((B, M)) * 0.4 * t),
            "w_second": bf(np.random.standard_normal((M, E)) * 1.4 / np.sqrt(E) / s[None, :]),
            "b_second": bf(np.random.standard_normal(M) * 0.3),
            "w_int": bf(np.random.standard_normal((M, E)) * 1.4 / np.sqrt(E) / s[None, :] * t[:, None]),
            "b_int": bf(np.random.standard_normal(M) * 0.3 * t),
            "w_out": bf(np.random.standard_normal((V, M)) / np.sqrt(M) / t[None, :]),
            "b_out": bf(np.random.standard_normal(V) * 0.3)}


def reference(y2, first, w_second, b_second, w_int, b_int, w_out, b_out):
    y2q = mxq(f64(y2), 1, "e4m3")
    second = np.maximum((y2q @ mxq(f64(w_second), 1, "e4m3").T) + f64(b_second), 0.0)
    inter = np.maximum((y2q @ mxq(f64(w_int), 1, "e4m3").T) + f64(b_int), 0.0)
    z = second * f64(first) + inter
    return (mxq(z, 1, "e4m3") @ mxq(f64(w_out), 1, "e4m3").T) + f64(b_out)

@@ -1,0 +1,285 @@
+from contextlib import ExitStack
+
+import concourse.mybir as mybir
+from concourse.masks import make_identity
+
+F32 = mybir.dt.float32
+BF16 = mybir.dt.bfloat16
+U32 = mybir.dt.uint32
+U8 = mybir.dt.uint8
+FP8X4 = mybir.dt.float8_e4m3fn_x4
+RELU = mybir.ActivationFunctionType.Relu
+ADD = mybir.AluOpType.add
+MULT = mybir.AluOpType.mult
+
+P = 128
+PACK = 4
+K_PASS = P * PACK
+B, E, M, V = 512, 512, 1024, 4096
+B_TILES = B // P
+CHUNKS = M // P
+Z_PASSES = M // K_PASS
+V_BLOCK = 512
+V_BLOCKS = V // V_BLOCK
+V_TILES = V_BLOCK // P
+V_STORE = 2 * V_BLOCK
+
+FLOPS = 2 * B * E * M * 2 + 2 * B * M * V
+
+
+def k_to_partitions(nc, psum_t, ident, pieces, grouped, copies):
+    words = grouped.bitcast(F32)
+    for i in range(len(pieces) // 2):
+        bank = psum_t.tile([P, 2, 2, P], F32, tag="bank")
+        for a in range(2):
+            piece = pieces[2 * i + a].bitcast(F32)
+            for u in range(2):
+                nc.tensor.transpose(bank[:, a, u, :], piece[:, u * P : (u + 1) * P], ident)
+        copies[i % len(copies)](
+            out=words[:, 4 * P * i : 4 * P * (i + 1)].rearrange(
+                "p (a c u) -> p a c u", a=2, u=2
+            ),
+            in_=bank[:].rearrange("p a u c -> p a c u"),
+        )
+
+
+def tile_smcrossbaby_1_pb_kernel(
+    tc, y2, first, w_second, b_second, w_int, b_int, w_out, b_out, out
+):
+    nc = tc.nc
+    with ExitStack() as ctx:
+        const = ctx.enter_context(tc.tile_pool(name="const", bufs=1))
+        raw = ctx.enter_context(tc.tile_pool(name="raw", bufs=8))
+        group = ctx.enter_context(tc.tile_pool(name="group", bufs=3))
+        keep = ctx.enter_context(tc.tile_pool(name="keep", bufs=1))
+        psum_t = ctx.enter_context(tc.psum_pool(name="psum_t", bufs=4))
+        psum_acc = ctx.enter_context(tc.psum_pool(name="psum_acc", bufs=4))
+
+        ident = const.tile([P, P], F32)
+        make_identity(nc, ident[:])
+        ident_bf = const.tile([P, P], BF16)
+        make_identity(nc, ident_bf[:])
+        bo_rows = const.tile([P, V_BLOCK], BF16)
+        nc.vector.memset(bo_rows[:], 0.0)
+        bias_rows = const.tile([P, 2 * P], BF16)
+        nc.vector.memset(bias_rows[:], 0.0)
+
+        nc.sync.dma_start(
+            out=bo_rows[0:V_BLOCKS, :], in_=b_out.rearrange("(j n) -> j n", j=V_BLOCKS)
+        )
+        y2_raw = raw.tile([P, B_TILES, E], BF16, tag="raw")
+        nc.sync.dma_start(out=y2_raw[:], in_=y2.rearrange("(c r) k -> c r k", r=B_TILES))
+        w2_raw = raw.tile([P, 4, 2, E], BF16, tag="raw")
+        nc.sync.dma_start(
+            out=w2_raw[:], in_=w_second.rearrange("(q c e) k -> c q e k", q=4, e=2)
+        )
+        nc.sync.dma_start(out=bias_rows[0:4, :], in_=b_second.rearrange("(q x) -> q x", q=4))
+        nc.sync.dma_start(out=bias_rows[4:8, :], in_=b_int.rearrange("(q x) -> q x", q=4))
+        wi_raw = raw.tile([P, 4, 2, E], BF16, tag="raw")
+        nc.sync.dma_start(
+            out=wi_raw[:], in_=w_int.rearrange("(q c e) k -> c q e k", q=4, e=2)
+        )
+        first_raw = raw.tile([P, B_TILES, M], BF16, tag="raw")
+        nc.sync.dma_start(
+            out=first_raw[:], in_=first.rearrange("(c r) m -> c r m", r=B_TILES)
+        )
+        wo_raw = []
+        for j in range(V_BLOCKS):
+            wo_raw.append(raw.tile([P, V_TILES, M], BF16, tag="raw", name="wo_raw%d" % j))
+            nc.sync.dma_start(
+                out=wo_raw[j][:],
+                in_=w_out[j * V_BLOCK : (j + 1) * V_BLOCK, :].rearrange(
+                    "(c s) k -> c s k", s=V_TILES
+                ),
+            )
+
+        both = [nc.scalar.copy, nc.vector.tensor_copy]
+
+        bo = const.tile([P, V], BF16)
+        for j in range(V_BLOCKS):
+            acc = psum_acc.tile([P, V_BLOCK], F32, tag="acc")
+            nc.tensor.matmul(
+                out=acc[:],
+                lhsT=ident_bf[:, j : j + 1].to_broadcast([P, P]),
+                rhs=bo_rows[:],
+                start=True,
+                stop=True,
+            )
+            both[j % 2](out=bo[:, j * V_BLOCK : (j + 1) * V_BLOCK], in_=acc[:])
+
+        y2_c = keep.tile([P, B], U32, align_bytes=64)
+        y2_s = keep.tile([P, B], U8, align_bytes=64)
+        w2_c = keep.tile([P, M], U32, align_bytes=64)
+        w2_s = keep.tile([P, M], U8, align_bytes=64)
+        wi_c = keep.tile([P, M], U32, align_bytes=64)
+        wi_s = keep.tile([P, M], U8, align_bytes=64)
+
+        y2_g = group.tile([P, B * PACK], BF16, tag="group", align_bytes=64)
+        k_to_partitions(
+            nc, psum_t, ident[:], [y2_raw[:, r, :] for r in range(B_TILES)], y2_g[:], both
+        )
+        w2_g = group.tile([P, M * PACK], BF16, tag="group", align_bytes=64)
+        k_to_partitions(
+            nc,
+            psum_t,
+            ident[:],
+            [w2_raw[:, q, e, :] for q in range(4) for e in range(2)],
+            w2_g[:],
+            both,
+        )
+        nc.vector.quantize_mx(out=y2_c[:].bitcast(FP8X4), scales=y2_s[:], in_=y2_g[:])
+        nc.vector.quantize_mx(out=w2_c[:].bitcast(FP8X4), scales=w2_s[:], in_=w2_g[:])
+
+        bias_split = const.tile([P, 2, P], F32)
+        nc.vector.tensor_copy(
+            out=bias_split[:], in_=bias_rows[:].rearrange("p (c e) -> p e c", e=2)
+        )
+        bias_t = psum_t.tile([P, 2, 2, P], F32, tag="bank")
+        for e in range(2):
+            nc.tensor.transpose(bias_t[:, 0, e, :], bias_split[:, e, :], ident[:])
+        bias = const.tile([P, 2, CHUNKS], F32)
+        nc.vector.tensor_copy(
+            out=bias[:].rearrange("p w (q e) -> p w q e", e=2),
+            in_=bias_t[:, 0, :, 0:8].rearrange("p e (w q) -> p w q e", w=2),
+        )
+
+        wi_g = group.tile([P, M * PACK], BF16, tag="group", align_bytes=64)
+        k_to_partitions(
+            nc,
+            psum_t,
+            ident[:],
+            [wi_raw[:, q, e, :] for q in range(4) for e in range(2)],
+            wi_g[:],
+            both,
+        )
+        nc.vector.quantize_mx(out=wi_c[:].bitcast(FP8X4), scales=wi_s[:], in_=wi_g[:])
+
+        z_c = keep.tile([P, Z_PASSES, B], U32, align_bytes=64)
+        z_s = keep.tile([P, Z_PASSES, B], U8, align_bytes=64)
+
+        with tc.tile_pool(name="hidden", bufs=1) as hidden:
+            second = hidden.tile([P, CHUNKS, B], F32)
+            inter = hidden.tile([P, CHUNKS, B], F32)
+            for chunk in range(CHUNKS):
+                cols = slice(chunk * P, (chunk + 1) * P)
+                acc = psum_acc.tile([P, B], F32, tag="acc")
+                nc.tensor.matmul_mx(
+                    out=acc[:],
+                    lhsT=w2_c[:, cols].bitcast(FP8X4),
+                    lhsT_scale=w2_s[:, cols],
+                    rhs=y2_c[:].bitcast(FP8X4),
+                    rhs_scale=y2_s[:],
+                    start=True,
+                    stop=True,
+                )
+                nc.scalar.activation(
+                    out=second[:, chunk, :],
+                    in_=acc[:],
+                    func=RELU,
+                    bias=bias[:, 0, chunk : chunk + 1],
+                )
+            for chunk in range(CHUNKS):
+                cols = slice(chunk * P, (chunk + 1) * P)
+                acc = psum_acc.tile([P, B], F32, tag="acc")
+                nc.tensor.matmul_mx(
+                    out=acc[:],
+                    lhsT=wi_c[:, cols].bitcast(FP8X4),
+                    lhsT_scale=wi_s[:, cols],
+                    rhs=y2_c[:].bitcast(FP8X4),
+                    rhs_scale=y2_s[:],
+                    start=True,
+                    stop=True,
+                )
+                nc.scalar.activation(
+                    out=inter[:, chunk, :],
+                    in_=acc[:],
+                    func=RELU,
+                    bias=bias[:, 1, chunk : chunk + 1],
+                )
+            for q in range(4):
+                first_t = psum_t.tile([P, B], F32, tag="bank")
+                for r in range(B_TILES):
+                    nc.tensor.transpose(
+                        first_t[:, r * P : (r + 1) * P],
+                        first_raw[:, r, :].bitcast(F32)[:, q * P : (q + 1) * P],
+                        ident[:],
+                    )
+                nc.vector.tensor_tensor(
+                    out=second[:, 2 * q : 2 * q + 2, :],
+                    in0=second[:, 2 * q : 2 * q + 2, :],
+                    in1=first_t[:].bitcast(BF16).rearrange("p (n e) -> p e n", e=2),
+                    op=MULT,
+                )
+            for g in range(Z_PASSES):
+                z_g = hidden.tile([P, B * PACK], BF16, align_bytes=64, name="z_g%d" % g)
+                nc.vector.tensor_tensor(
+                    out=z_g[:].rearrange("p (n t) -> p n t", t=PACK),
+                    in0=second[:, PACK * g : PACK * (g + 1), :].rearrange("p t n -> p n t"),
+                    in1=inter[:, PACK * g : PACK * (g + 1), :].rearrange("p t n -> p n t"),
+                    op=ADD,
+                )
+                nc.vector.quantize_mx(
+                    out=z_c[:, g, :].bitcast(FP8X4), scales=z_s[:, g, :], in_=z_g[:]
+                )
+
+        wo_c = keep.tile([P, V_BLOCKS, Z_PASSES, V_BLOCK], U32, align_bytes=64)
+        wo_s = keep.tile([P, V_BLOCKS, Z_PASSES, V_BLOCK], U8, align_bytes=64)
+        out_rows = out.rearrange("(c r) v -> c r v", r=B_TILES)
+
+        def prepare_block(j):
+            wo_g = group.tile([P, Z_PASSES * V_BLOCK * PACK], BF16, tag="group", align_bytes=64)
+            k_to_partitions(
+                nc,
+                psum_t,
+                ident[:],
+                [
+                    wo_raw[j][:, s, g * K_PASS : (g + 1) * K_PASS]
+                    for g in range(Z_PASSES)
+                    for s in range(V_TILES)
+                ],
+                wo_g[:],
+                [nc.scalar.copy],
+            )
+            nc.vector.quantize_mx(
+                out=wo_c[:, j, :, :].rearrange("p g n -> p (g n)").bitcast(FP8X4),
+                scales=wo_s[:, j, :, :].rearrange("p g n -> p (g n)"),
+                in_=wo_g[:],
+            )
+
+        with tc.tile_pool(name="result", bufs=2 * B_TILES) as result:
+            prepare_block(0)
+            res = [None] * B_TILES
+            for j in range(V_BLOCKS):
+                if j + 1 < V_BLOCKS:
+                    prepare_block(j + 1)
+                half = j % 2
+                for r in range(B_TILES):
+                    rows = slice(r * P, (r + 1) * P)
+                    acc = psum_acc.tile([P, V_BLOCK], F32, tag="acc")
+                    for g in range(Z_PASSES):
+                        nc.tensor.matmul_mx(
+                            out=acc[:],
+                            lhsT=z_c[:, g, rows].bitcast(FP8X4),
+                            lhsT_scale=z_s[:, g, rows],
+                            rhs=wo_c[:, j, g, :].bitcast(FP8X4),
+                            rhs_scale=wo_s[:, j, g, :],
+                            start=(g == 0),
+                            stop=(g == Z_PASSES - 1),
+                        )
+                    if half == 0:
+                        res[r] = result.tile([P, V_STORE], F32, tag="res", name="res%d" % r)
+                    nc.vector.tensor_tensor(
+                        out=res[r][:, half * V_BLOCK : (half + 1) * V_BLOCK].rearrange(
+                            "p (c s) -> p c s", s=V_TILES
+                        ),
+                        in0=acc[:].rearrange("p (s c) -> p c s", s=V_TILES),
+                        in1=bo[:, j * V_BLOCK : (j + 1) * V_BLOCK].rearrange(
+                            "p (c s) -> p c s", s=V_TILES
+                        ),
+                        op=ADD,
+                    )
+                    if half == 1:
+                        nc.sync.dma_start(
+                            out=out_rows[:, r, (j - 1) * V_BLOCK : (j + 1) * V_BLOCK],
+                            in_=res[r][:],
+                        )

@@ -23,6 +23,7 @@ V_BLOCK = 512
 V_BLOCKS = V // V_BLOCK
 V_TILES = V_BLOCK // P
 V_STORE = 2 * V_BLOCK
+ACC_BANKS = 4
 
 FLOPS = 2 * B * E * M * 2 + 2 * B * M * V
 
@@ -53,7 +54,8 @@ def tile_smcrossbaby_1_pb_kernel(
         group = ctx.enter_context(tc.tile_pool(name="group", bufs=3))
         keep = ctx.enter_context(tc.tile_pool(name="keep", bufs=1))
         psum_t = ctx.enter_context(tc.psum_pool(name="psum_t", bufs=4))
-        psum_acc = ctx.enter_context(tc.psum_pool(name="psum_acc", bufs=4))
+        psum_acc = ctx.enter_context(tc.psum_pool(name="psum_acc", bufs=ACC_BANKS))
+        ctx.enter_context(tc.manual_schedule())
 
         ident = const.tile([P, P], F32)
         make_identity(nc, ident[:])
@@ -67,14 +69,14 @@ def tile_smcrossbaby_1_pb_kernel(
         nc.sync.dma_start(
             out=bo_rows[0:V_BLOCKS, :], in_=b_out.rearrange("(j n) -> j n", j=V_BLOCKS)
         )
+        nc.sync.dma_start(out=bias_rows[0:4, :], in_=b_second.rearrange("(q x) -> q x", q=4))
+        nc.sync.dma_start(out=bias_rows[4:8, :], in_=b_int.rearrange("(q x) -> q x", q=4))
         y2_raw = raw.tile([P, B_TILES, E], BF16, tag="raw")
         nc.sync.dma_start(out=y2_raw[:], in_=y2.rearrange("(c r) k -> c r k", r=B_TILES))
         w2_raw = raw.tile([P, 4, 2, E], BF16, tag="raw")
         nc.sync.dma_start(
             out=w2_raw[:], in_=w_second.rearrange("(q c e) k -> c q e k", q=4, e=2)
         )
-        nc.sync.dma_start(out=bias_rows[0:4, :], in_=b_second.rearrange("(q x) -> q x", q=4))
-        nc.sync.dma_start(out=bias_rows[4:8, :], in_=b_int.rearrange("(q x) -> q x", q=4))
         wi_raw = raw.tile([P, 4, 2, E], BF16, tag="raw")
         nc.sync.dma_start(
             out=wi_raw[:], in_=w_int.rearrange("(q c e) k -> c q e k", q=4, e=2)
@@ -107,29 +109,6 @@ def tile_smcrossbaby_1_pb_kernel(
             )
             both[j % 2](out=bo[:, j * V_BLOCK : (j + 1) * V_BLOCK], in_=acc[:])
 
-        y2_c = keep.tile([P, B], U32, align_bytes=64)
-        y2_s = keep.tile([P, B], U8, align_bytes=64)
-        w2_c = keep.tile([P, M], U32, align_bytes=64)
-        w2_s = keep.tile([P, M], U8, align_bytes=64)
-        wi_c = keep.tile([P, M], U32, align_bytes=64)
-        wi_s = keep.tile([P, M], U8, align_bytes=64)
-
-        y2_g = group.tile([P, B * PACK], BF16, tag="group", align_bytes=64)
-        k_to_partitions(
-            nc, psum_t, ident[:], [y2_raw[:, r, :] for r in range(B_TILES)], y2_g[:], both
-        )
-        w2_g = group.tile([P, M * PACK], BF16, tag="group", align_bytes=64)
-        k_to_partitions(
-            nc,
-            psum_t,
-            ident[:],
-            [w2_raw[:, q, e, :] for q in range(4) for e in range(2)],
-            w2_g[:],
-            both,
-        )
-        nc.vector.quantize_mx(out=y2_c[:].bitcast(FP8X4), scales=y2_s[:], in_=y2_g[:])
-        nc.vector.quantize_mx(out=w2_c[:].bitcast(FP8X4), scales=w2_s[:], in_=w2_g[:])
-
         bias_split = const.tile([P, 2, P], F32)
         nc.vector.tensor_copy(
             out=bias_split[:], in_=bias_rows[:].rearrange("p (c e) -> p e c", e=2)
@@ -143,91 +122,44 @@ def tile_smcrossbaby_1_pb_kernel(
             in_=bias_t[:, 0, :, 0:8].rearrange("p e (w q) -> p w q e", w=2),
         )
 
-        wi_g = group.tile([P, M * PACK], BF16, tag="group", align_bytes=64)
+        y2_c = keep.tile([P, B], U32, align_bytes=64)
+        y2_s = keep.tile([P, B], U8, align_bytes=64)
+        w2_c = keep.tile([P, M], U32, align_bytes=64)
+        w2_s = keep.tile([P, M], U8, align_bytes=64)
+        wi_c = keep.tile([P, M], U32, align_bytes=64)
+        wi_s = keep.tile([P, M], U8, align_bytes=64)
+
+        def quantise(codes, scales, grouped):
+            nc.vector.quantize_mx(out=codes.bitcast(FP8X4), scales=scales, in_=grouped)
+
+        y2_g = group.tile([P, B * PACK], BF16, tag="group", align_bytes=64)
         k_to_partitions(
-            nc,
-            psum_t,
-            ident[:],
-            [wi_raw[:, q, e, :] for q in range(4) for e in range(2)],
-            wi_g[:],
-            both,
+            nc, psum_t, ident[:], [y2_raw[:, r, :] for r in range(B_TILES)], y2_g[:], both
         )
-        nc.vector.quantize_mx(out=wi_c[:].bitcast(FP8X4), scales=wi_s[:], in_=wi_g[:])
+        w2_g = group.tile([P, 2, M * PACK // 2], BF16, tag="group", align_bytes=64)
+        wi_g = group.tile([P, 2, M * PACK // 2], BF16, tag="group", align_bytes=64)
+        w2_rows = [w2_raw[:, q, e, :] for q in range(4) for e in range(2)]
+        wi_rows = [wi_raw[:, q, e, :] for q in range(4) for e in range(2)]
+        k_to_partitions(nc, psum_t, ident[:], w2_rows[0:4], w2_g[:, 0, :], both)
+        quantise(y2_c[:], y2_s[:], y2_g[:])
+        k_to_partitions(nc, psum_t, ident[:], w2_rows[4:8], w2_g[:, 1, :], both)
+        quantise(w2_c[:, 0 : M // 2], w2_s[:, 0 : M // 2], w2_g[:, 0, :])
+        k_to_partitions(nc, psum_t, ident[:], wi_rows[0:4], wi_g[:, 0, :], both)
+        quantise(w2_c[:, M // 2 : M], w2_s[:, M // 2 : M], w2_g[:, 1, :])
+        k_to_partitions(nc, psum_t, ident[:], wi_rows[4:8], wi_g[:, 1, :], both)
+        quantise(wi_c[:, 0 : M // 2], wi_s[:, 0 : M // 2], wi_g[:, 0, :])
+        quantise(wi_c[:, M // 2 : M], wi_s[:, M // 2 : M], wi_g[:, 1, :])
 
         z_c = keep.tile([P, Z_PASSES, B], U32, align_bytes=64)
         z_s = keep.tile([P, Z_PASSES, B], U8, align_bytes=64)
-
-        with tc.tile_pool(name="hidden", bufs=1) as hidden:
-            second = hidden.tile([P, CHUNKS, B], F32)
-            inter = hidden.tile([P, CHUNKS, B], F32)
-            for chunk in range(CHUNKS):
-                cols = slice(chunk * P, (chunk + 1) * P)
-                acc = psum_acc.tile([P, B], F32, tag="acc")
-                nc.tensor.matmul_mx(
-                    out=acc[:],
-                    lhsT=w2_c[:, cols].bitcast(FP8X4),
-                    lhsT_scale=w2_s[:, cols],
-                    rhs=y2_c[:].bitcast(FP8X4),
-                    rhs_scale=y2_s[:],
-                    start=True,
-                    stop=True,
-                )
-                nc.scalar.activation(
-                    out=second[:, chunk, :],
-                    in_=acc[:],
-                    func=RELU,
-                    bias=bias[:, 0, chunk : chunk + 1],
-                )
-            for chunk in range(CHUNKS):
-                cols = slice(chunk * P, (chunk + 1) * P)
-                acc = psum_acc.tile([P, B], F32, tag="acc")
-                nc.tensor.matmul_mx(
-                    out=acc[:],
-                    lhsT=wi_c[:, cols].bitcast(FP8X4),
-                    lhsT_scale=wi_s[:, cols],
-                    rhs=y2_c[:].bitcast(FP8X4),
-                    rhs_scale=y2_s[:],
-                    start=True,
-                    stop=True,
-                )
-                nc.scalar.activation(
-                    out=inter[:, chunk, :],
-                    in_=acc[:],
-                    func=RELU,
-                    bias=bias[:, 1, chunk : chunk + 1],
-                )
-            for q in range(4):
-                first_t = psum_t.tile([P, B], F32, tag="bank")
-                for r in range(B_TILES):
-                    nc.tensor.transpose(
-                        first_t[:, r * P : (r + 1) * P],
-                        first_raw[:, r, :].bitcast(F32)[:, q * P : (q + 1) * P],
-                        ident[:],
-                    )
-                nc.vector.tensor_tensor(
-                    out=second[:, 2 * q : 2 * q + 2, :],
-                    in0=second[:, 2 * q : 2 * q + 2, :],
-                    in1=first_t[:].bitcast(BF16).rearrange("p (n e) -> p e n", e=2),
-                    op=MULT,
-                )
-            for g in range(Z_PASSES):
-                z_g = hidden.tile([P, B * PACK], BF16, align_bytes=64, name="z_g%d" % g)
-                nc.vector.tensor_tensor(
-                    out=z_g[:].rearrange("p (n t) -> p n t", t=PACK),
-                    in0=second[:, PACK * g : PACK * (g + 1), :].rearrange("p t n -> p n t"),
-                    in1=inter[:, PACK * g : PACK * (g + 1), :].rearrange("p t n -> p n t"),
-                    op=ADD,
-                )
-                nc.vector.quantize_mx(
-                    out=z_c[:, g, :].bitcast(FP8X4), scales=z_s[:, g, :], in_=z_g[:]
-                )
-
         wo_c = keep.tile([P, V_BLOCKS, Z_PASSES, V_BLOCK], U32, align_bytes=64)
         wo_s = keep.tile([P, V_BLOCKS, Z_PASSES, V_BLOCK], U8, align_bytes=64)
-        out_rows = out.rearrange("(c r) v -> c r v", r=B_TILES)
+        wo_g = [None] * V_BLOCKS
 
-        def prepare_block(j):
-            wo_g = group.tile([P, Z_PASSES * V_BLOCK * PACK], BF16, tag="group", align_bytes=64)
+        def transpose_block(j):
+            wo_g[j] = group.tile(
+                [P, Z_PASSES * V_BLOCK * PACK], BF16, tag="group", align_bytes=64, name="wo_g%d" % j
+            )
             k_to_partitions(
                 nc,
                 psum_t,
@@ -237,21 +169,80 @@ def tile_smcrossbaby_1_pb_kernel(
                     for g in range(Z_PASSES)
                     for s in range(V_TILES)
                 ],
-                wo_g[:],
+                wo_g[j][:],
                 [nc.scalar.copy],
             )
-            nc.vector.quantize_mx(
-                out=wo_c[:, j, :, :].rearrange("p g n -> p (g n)").bitcast(FP8X4),
-                scales=wo_s[:, j, :, :].rearrange("p g n -> p (g n)"),
-                in_=wo_g[:],
+
+        def quantise_block(j):
+            quantise(
+                wo_c[:, j, :, :].rearrange("p g n -> p (g n)"),
+                wo_s[:, j, :, :].rearrange("p g n -> p (g n)"),
+                wo_g[j][:],
             )
 
+        def hidden_layer(w_c, w_s, chunk, bias_col, result):
+            cols = slice(chunk * P, (chunk + 1) * P)
+            acc = psum_acc.tile([P, B], F32, tag="acc")
+            nc.tensor.matmul_mx(
+                out=acc[:],
+                lhsT=w_c[:, cols].bitcast(FP8X4),
+                lhsT_scale=w_s[:, cols],
+                rhs=y2_c[:].bitcast(FP8X4),
+                rhs_scale=y2_s[:],
+                start=True,
+                stop=True,
+            )
+            nc.scalar.activation(out=result, in_=acc[:], func=RELU, bias=bias_col)
+
+        with tc.tile_pool(name="hidden", bufs=1) as hidden:
+            second = hidden.tile([P, CHUNKS, B], F32)
+            inter = hidden.tile([P, CHUNKS, B], F32)
+            z_g = hidden.tile([P, Z_PASSES, B * PACK], BF16, align_bytes=64)
+            first_t = []
+            for chunk in range(CHUNKS):
+                if chunk == ACC_BANKS:
+                    for q in range(4):
+                        first_t.append(psum_t.tile([P, B], F32, tag="bank", name="first_t%d" % q))
+                        for r in range(B_TILES):
+                            nc.tensor.transpose(
+                                first_t[q][:, r * P : (r + 1) * P],
+                                first_raw[:, r, :].bitcast(F32)[:, q * P : (q + 1) * P],
+                                ident[:],
+                            )
+                hidden_layer(w2_c, w2_s, chunk, bias[:, 0, chunk : chunk + 1], second[:, chunk, :])
+            for q in range(4):
+                nc.vector.tensor_tensor(
+                    out=second[:, 2 * q : 2 * q + 2, :],
+                    in0=second[:, 2 * q : 2 * q + 2, :],
+                    in1=first_t[q][:].bitcast(BF16).rearrange("p (n e) -> p e n", e=2),
+                    op=MULT,
+                )
+            for chunk in range(CHUNKS):
+                hidden_layer(wi_c, wi_s, chunk, bias[:, 1, chunk : chunk + 1], inter[:, chunk, :])
+            transpose_block(0)
+            transpose_block(1)
+            for g in range(Z_PASSES):
+                nc.vector.tensor_tensor(
+                    out=z_g[:, g, :].rearrange("p (n t) -> p n t", t=PACK),
+                    in0=second[:, PACK * g : PACK * (g + 1), :].rearrange("p t n -> p n t"),
+                    in1=inter[:, PACK * g : PACK * (g + 1), :].rearrange("p t n -> p n t"),
+                    op=ADD,
+                )
+            quantise_block(0)
+            quantise(
+                z_c[:].rearrange("p g n -> p (g n)"),
+                z_s[:].rearrange("p g n -> p (g n)"),
+                z_g[:].rearrange("p g x -> p (g x)"),
+            )
+
+        out_rows = out.rearrange("(c r) v -> c r v", r=B_TILES)
         with tc.tile_pool(name="result", bufs=2 * B_TILES) as result:
-            prepare_block(0)
             res = [None] * B_TILES
             for j in range(V_BLOCKS):
                 if j + 1 < V_BLOCKS:
-                    prepare_block(j + 1)
+                    quantise_block(j + 1)
+                if j + 2 < V_BLOCKS:
+                    transpose_block(j + 2)
                 half = j % 2
                 for r in range(B_TILES):
                     rows = slice(r * P, (r + 1) * P)

@@ -22,7 +22,6 @@ Z_PASSES = M // K_PASS
 V_BLOCK = 512
 V_BLOCKS = V // V_BLOCK
 V_TILES = V_BLOCK // P
-V_STORE = 2 * V_BLOCK
 ACC_BANKS = 4
 
 FLOPS = 2 * B * E * M * 2 + 2 * B * M * V
@@ -91,23 +90,11 @@ def tile_smcrossbaby_1_pb_kernel(
             nc.sync.dma_start(
                 out=wo_raw[j][:],
                 in_=w_out[j * V_BLOCK : (j + 1) * V_BLOCK, :].rearrange(
-                    "(c s) k -> c s k", s=V_TILES
+                    "(s c) k -> c s k", s=V_TILES
                 ),
             )
 
         both = [nc.scalar.copy, nc.vector.tensor_copy]
-
-        bo = const.tile([P, V], BF16)
-        for j in range(V_BLOCKS):
-            acc = psum_acc.tile([P, V_BLOCK], F32, tag="acc")
-            nc.tensor.matmul(
-                out=acc[:],
-                lhsT=ident_bf[:, j : j + 1].to_broadcast([P, P]),
-                rhs=bo_rows[:],
-                start=True,
-                stop=True,
-            )
-            both[j % 2](out=bo[:, j * V_BLOCK : (j + 1) * V_BLOCK], in_=acc[:])
 
         bias_split = const.tile([P, 2, P], F32)
         nc.vector.tensor_copy(
@@ -122,6 +109,24 @@ def tile_smcrossbaby_1_pb_kernel(
             in_=bias_t[:, 0, :, 0:8].rearrange("p e (w q) -> p w q e", w=2),
         )
 
+        bo = const.tile([P, V], BF16)
+
+        def spread_b_out(pair):
+            spread = psum_acc.tile([P, 2, V_BLOCK], BF16, tag="acc")
+            for i in range(2):
+                j = 2 * pair + i
+                nc.tensor.matmul(
+                    out=spread[:, i, :],
+                    lhsT=ident_bf[:, j : j + 1].to_broadcast([P, P]),
+                    rhs=bo_rows[:],
+                    start=True,
+                    stop=True,
+                )
+            nc.scalar.copy(
+                out=bo[:, 2 * pair * V_BLOCK : 2 * (pair + 1) * V_BLOCK],
+                in_=spread[:].rearrange("p i n -> p (i n)"),
+            )
+
         y2_c = keep.tile([P, B], U32, align_bytes=64)
         y2_s = keep.tile([P, B], U8, align_bytes=64)
         w2_c = keep.tile([P, M], U32, align_bytes=64)
@@ -133,22 +138,27 @@ def tile_smcrossbaby_1_pb_kernel(
             nc.vector.quantize_mx(out=codes.bitcast(FP8X4), scales=scales, in_=grouped)
 
         y2_g = group.tile([P, B * PACK], BF16, tag="group", align_bytes=64)
-        k_to_partitions(
-            nc, psum_t, ident[:], [y2_raw[:, r, :] for r in range(B_TILES)], y2_g[:], both
-        )
         w2_g = group.tile([P, 2, M * PACK // 2], BF16, tag="group", align_bytes=64)
         wi_g = group.tile([P, 2, M * PACK // 2], BF16, tag="group", align_bytes=64)
         w2_rows = [w2_raw[:, q, e, :] for q in range(4) for e in range(2)]
         wi_rows = [wi_raw[:, q, e, :] for q in range(4) for e in range(2)]
-        k_to_partitions(nc, psum_t, ident[:], w2_rows[0:4], w2_g[:, 0, :], both)
+        spread_b_out(0)
+        spread_b_out(1)
+        k_to_partitions(
+            nc,
+            psum_t,
+            ident[:],
+            [y2_raw[:, r, :] for r in range(B_TILES)],
+            y2_g[:],
+            [nc.scalar.copy],
+        )
         quantise(y2_c[:], y2_s[:], y2_g[:])
-        k_to_partitions(nc, psum_t, ident[:], w2_rows[4:8], w2_g[:, 1, :], both)
+        spread_b_out(2)
+        spread_b_out(3)
+        k_to_partitions(nc, psum_t, ident[:], w2_rows[0:4], w2_g[:, 0, :], [nc.scalar.copy])
+        k_to_partitions(nc, psum_t, ident[:], w2_rows[4:8], w2_g[:, 1, :], [nc.scalar.copy])
         quantise(w2_c[:, 0 : M // 2], w2_s[:, 0 : M // 2], w2_g[:, 0, :])
-        k_to_partitions(nc, psum_t, ident[:], wi_rows[0:4], wi_g[:, 0, :], both)
         quantise(w2_c[:, M // 2 : M], w2_s[:, M // 2 : M], w2_g[:, 1, :])
-        k_to_partitions(nc, psum_t, ident[:], wi_rows[4:8], wi_g[:, 1, :], both)
-        quantise(wi_c[:, 0 : M // 2], wi_s[:, 0 : M // 2], wi_g[:, 0, :])
-        quantise(wi_c[:, M // 2 : M], wi_s[:, M // 2 : M], wi_g[:, 1, :])
 
         z_c = keep.tile([P, Z_PASSES, B], U32, align_bytes=64)
         z_s = keep.tile([P, Z_PASSES, B], U8, align_bytes=64)
@@ -198,18 +208,23 @@ def tile_smcrossbaby_1_pb_kernel(
             second = hidden.tile([P, CHUNKS, B], F32)
             inter = hidden.tile([P, CHUNKS, B], F32)
             z_g = hidden.tile([P, Z_PASSES, B * PACK], BF16, align_bytes=64)
-            first_t = []
-            for chunk in range(CHUNKS):
-                if chunk == ACC_BANKS:
-                    for q in range(4):
-                        first_t.append(psum_t.tile([P, B], F32, tag="bank", name="first_t%d" % q))
-                        for r in range(B_TILES):
-                            nc.tensor.transpose(
-                                first_t[q][:, r * P : (r + 1) * P],
-                                first_raw[:, r, :].bitcast(F32)[:, q * P : (q + 1) * P],
-                                ident[:],
-                            )
+            for chunk in range(ACC_BANKS):
                 hidden_layer(w2_c, w2_s, chunk, bias[:, 0, chunk : chunk + 1], second[:, chunk, :])
+            k_to_partitions(nc, psum_t, ident[:], wi_rows[0:4], wi_g[:, 0, :], both)
+            k_to_partitions(nc, psum_t, ident[:], wi_rows[4:8], wi_g[:, 1, :], both)
+            for chunk in range(ACC_BANKS, CHUNKS):
+                hidden_layer(w2_c, w2_s, chunk, bias[:, 0, chunk : chunk + 1], second[:, chunk, :])
+            quantise(wi_c[:, 0 : M // 2], wi_s[:, 0 : M // 2], wi_g[:, 0, :])
+            quantise(wi_c[:, M // 2 : M], wi_s[:, M // 2 : M], wi_g[:, 1, :])
+            first_t = []
+            for q in range(4):
+                first_t.append(psum_t.tile([P, B], F32, tag="bank", name="first_t%d" % q))
+                for r in range(B_TILES):
+                    nc.tensor.transpose(
+                        first_t[q][:, r * P : (r + 1) * P],
+                        first_raw[:, r, :].bitcast(F32)[:, q * P : (q + 1) * P],
+                        ident[:],
+                    )
             for q in range(4):
                 nc.vector.tensor_tensor(
                     out=second[:, 2 * q : 2 * q + 2, :],
@@ -237,13 +252,12 @@ def tile_smcrossbaby_1_pb_kernel(
 
         out_rows = out.rearrange("(c r) v -> c r v", r=B_TILES)
         with tc.tile_pool(name="result", bufs=2 * B_TILES) as result:
-            res = [None] * B_TILES
             for j in range(V_BLOCKS):
                 if j + 1 < V_BLOCKS:
                     quantise_block(j + 1)
                 if j + 2 < V_BLOCKS:
                     transpose_block(j + 2)
-                half = j % 2
+                cols = slice(j * V_BLOCK, (j + 1) * V_BLOCK)
                 for r in range(B_TILES):
                     rows = slice(r * P, (r + 1) * P)
                     acc = psum_acc.tile([P, V_BLOCK], F32, tag="acc")
@@ -257,20 +271,6 @@ def tile_smcrossbaby_1_pb_kernel(
                             start=(g == 0),
                             stop=(g == Z_PASSES - 1),
                         )
-                    if half == 0:
-                        res[r] = result.tile([P, V_STORE], F32, tag="res", name="res%d" % r)
-                    nc.vector.tensor_tensor(
-                        out=res[r][:, half * V_BLOCK : (half + 1) * V_BLOCK].rearrange(
-                            "p (c s) -> p c s", s=V_TILES
-                        ),
-                        in0=acc[:].rearrange("p (s c) -> p c s", s=V_TILES),
-                        in1=bo[:, j * V_BLOCK : (j + 1) * V_BLOCK].rearrange(
-                            "p (c s) -> p c s", s=V_TILES
-                        ),
-                        op=ADD,
-                    )
-                    if half == 1:
-                        nc.sync.dma_start(
-                            out=out_rows[:, r, (j - 1) * V_BLOCK : (j + 1) * V_BLOCK],
-                            in_=res[r][:],
-                        )
+                    res = result.tile([P, V_BLOCK], F32)
+                    nc.vector.tensor_tensor(out=res[:], in0=acc[:], in1=bo[:, cols], op=ADD)
+                    nc.sync.dma_start(out=out_rows[:, r, cols], in_=res[:])

@@ -65,9 +65,6 @@ def tile_smcrossbaby_1_pb_kernel(
         bias_rows = const.tile([P, 2 * P], BF16)
         nc.vector.memset(bias_rows[:], 0.0)
 
-        nc.sync.dma_start(
-            out=bo_rows[0:V_BLOCKS, :], in_=b_out.rearrange("(j n) -> j n", j=V_BLOCKS)
-        )
         nc.sync.dma_start(out=bias_rows[0:4, :], in_=b_second.rearrange("(q x) -> q x", q=4))
         nc.sync.dma_start(out=bias_rows[4:8, :], in_=b_int.rearrange("(q x) -> q x", q=4))
         y2_raw = raw.tile([P, B_TILES, E], BF16, tag="raw")
@@ -75,6 +72,9 @@ def tile_smcrossbaby_1_pb_kernel(
         w2_raw = raw.tile([P, 4, 2, E], BF16, tag="raw")
         nc.sync.dma_start(
             out=w2_raw[:], in_=w_second.rearrange("(q c e) k -> c q e k", q=4, e=2)
+        )
+        nc.sync.dma_start(
+            out=bo_rows[0:V_BLOCKS, :], in_=b_out.rearrange("(j n) -> j n", j=V_BLOCKS)
         )
         wi_raw = raw.tile([P, 4, 2, E], BF16, tag="raw")
         nc.sync.dma_start(
@@ -112,7 +112,7 @@ def tile_smcrossbaby_1_pb_kernel(
         bo = const.tile([P, V], BF16)
 
         def spread_b_out(pair):
-            spread = psum_acc.tile([P, 2, V_BLOCK], BF16, tag="acc")
+            spread = psum_t.tile([P, 2, V_BLOCK], BF16, tag="bank")
             for i in range(2):
                 j = 2 * pair + i
                 nc.tensor.matmul(
@@ -122,7 +122,7 @@ def tile_smcrossbaby_1_pb_kernel(
                     start=True,
                     stop=True,
                 )
-            nc.scalar.copy(
+            nc.vector.tensor_copy(
                 out=bo[:, 2 * pair * V_BLOCK : 2 * (pair + 1) * V_BLOCK],
                 in_=spread[:].rearrange("p i n -> p (i n)"),
             )
@@ -142,20 +142,11 @@ def tile_smcrossbaby_1_pb_kernel(
         wi_g = group.tile([P, 2, M * PACK // 2], BF16, tag="group", align_bytes=64)
         w2_rows = [w2_raw[:, q, e, :] for q in range(4) for e in range(2)]
         wi_rows = [wi_raw[:, q, e, :] for q in range(4) for e in range(2)]
-        spread_b_out(0)
-        spread_b_out(1)
         k_to_partitions(
-            nc,
-            psum_t,
-            ident[:],
-            [y2_raw[:, r, :] for r in range(B_TILES)],
-            y2_g[:],
-            [nc.scalar.copy],
+            nc, psum_t, ident[:], [y2_raw[:, r, :] for r in range(B_TILES)], y2_g[:], both
         )
         quantise(y2_c[:], y2_s[:], y2_g[:])
-        spread_b_out(2)
-        spread_b_out(3)
-        k_to_partitions(nc, psum_t, ident[:], w2_rows[0:4], w2_g[:, 0, :], [nc.scalar.copy])
+        k_to_partitions(nc, psum_t, ident[:], w2_rows[0:4], w2_g[:, 0, :], both)
         k_to_partitions(nc, psum_t, ident[:], w2_rows[4:8], w2_g[:, 1, :], [nc.scalar.copy])
         quantise(w2_c[:, 0 : M // 2], w2_s[:, 0 : M // 2], w2_g[:, 0, :])
         quantise(w2_c[:, M // 2 : M], w2_s[:, M // 2 : M], w2_g[:, 1, :])
@@ -210,6 +201,8 @@ def tile_smcrossbaby_1_pb_kernel(
             z_g = hidden.tile([P, Z_PASSES, B * PACK], BF16, align_bytes=64)
             for chunk in range(ACC_BANKS):
                 hidden_layer(w2_c, w2_s, chunk, bias[:, 0, chunk : chunk + 1], second[:, chunk, :])
+            for pair in range(V_BLOCKS // 2):
+                spread_b_out(pair)
             k_to_partitions(nc, psum_t, ident[:], wi_rows[0:4], wi_g[:, 0, :], both)
             k_to_partitions(nc, psum_t, ident[:], wi_rows[4:8], wi_g[:, 1, :], both)
             for chunk in range(ACC_BANKS, CHUNKS):

@@ -65,6 +65,9 @@ def tile_smcrossbaby_1_pb_kernel(
         bias_rows = const.tile([P, 2 * P], BF16)
         nc.vector.memset(bias_rows[:], 0.0)
 
+        nc.sync.dma_start(
+            out=bo_rows[0:V_BLOCKS, :], in_=b_out.rearrange("(j n) -> j n", j=V_BLOCKS)
+        )
         nc.sync.dma_start(out=bias_rows[0:4, :], in_=b_second.rearrange("(q x) -> q x", q=4))
         nc.sync.dma_start(out=bias_rows[4:8, :], in_=b_int.rearrange("(q x) -> q x", q=4))
         y2_raw = raw.tile([P, B_TILES, E], BF16, tag="raw")
@@ -72,9 +75,6 @@ def tile_smcrossbaby_1_pb_kernel(
         w2_raw = raw.tile([P, 4, 2, E], BF16, tag="raw")
         nc.sync.dma_start(
             out=w2_raw[:], in_=w_second.rearrange("(q c e) k -> c q e k", q=4, e=2)
-        )
-        nc.sync.dma_start(
-            out=bo_rows[0:V_BLOCKS, :], in_=b_out.rearrange("(j n) -> j n", j=V_BLOCKS)
         )
         wi_raw = raw.tile([P, 4, 2, E], BF16, tag="raw")
         nc.sync.dma_start(
@@ -112,7 +112,7 @@ def tile_smcrossbaby_1_pb_kernel(
         bo = const.tile([P, V], BF16)
 
         def spread_b_out(pair):
-            spread = psum_t.tile([P, 2, V_BLOCK], BF16, tag="bank")
+            spread = psum_acc.tile([P, 2, V_BLOCK], BF16, tag="acc")
             for i in range(2):
                 j = 2 * pair + i
                 nc.tensor.matmul(
@@ -122,7 +122,7 @@ def tile_smcrossbaby_1_pb_kernel(
                     start=True,
                     stop=True,
                 )
-            nc.vector.tensor_copy(
+            nc.scalar.copy(
                 out=bo[:, 2 * pair * V_BLOCK : 2 * (pair + 1) * V_BLOCK],
                 in_=spread[:].rearrange("p i n -> p (i n)"),
             )
@@ -142,11 +142,20 @@ def tile_smcrossbaby_1_pb_kernel(
         wi_g = group.tile([P, 2, M * PACK // 2], BF16, tag="group", align_bytes=64)
         w2_rows = [w2_raw[:, q, e, :] for q in range(4) for e in range(2)]
         wi_rows = [wi_raw[:, q, e, :] for q in range(4) for e in range(2)]
+        spread_b_out(0)
+        spread_b_out(1)
         k_to_partitions(
-            nc, psum_t, ident[:], [y2_raw[:, r, :] for r in range(B_TILES)], y2_g[:], both
+            nc,
+            psum_t,
+            ident[:],
+            [y2_raw[:, r, :] for r in range(B_TILES)],
+            y2_g[:],
+            [nc.scalar.copy],
         )
         quantise(y2_c[:], y2_s[:], y2_g[:])
-        k_to_partitions(nc, psum_t, ident[:], w2_rows[0:4], w2_g[:, 0, :], both)
+        spread_b_out(2)
+        spread_b_out(3)
+        k_to_partitions(nc, psum_t, ident[:], w2_rows[0:4], w2_g[:, 0, :], [nc.scalar.copy])
         k_to_partitions(nc, psum_t, ident[:], w2_rows[4:8], w2_g[:, 1, :], [nc.scalar.copy])
         quantise(w2_c[:, 0 : M // 2], w2_s[:, 0 : M // 2], w2_g[:, 0, :])
         quantise(w2_c[:, M // 2 : M], w2_s[:, M // 2 : M], w2_g[:, 1, :])
@@ -198,11 +207,10 @@ def tile_smcrossbaby_1_pb_kernel(
         with tc.tile_pool(name="hidden", bufs=1) as hidden:
             second = hidden.tile([P, CHUNKS, B], F32)
             inter = hidden.tile([P, CHUNKS, B], F32)
+            z_rows = hidden.tile([P, CHUNKS, B], BF16)
             z_g = hidden.tile([P, Z_PASSES, B * PACK], BF16, align_bytes=64)
             for chunk in range(ACC_BANKS):
                 hidden_layer(w2_c, w2_s, chunk, bias[:, 0, chunk : chunk + 1], second[:, chunk, :])
-            for pair in range(V_BLOCKS // 2):
-                spread_b_out(pair)
             k_to_partitions(nc, psum_t, ident[:], wi_rows[0:4], wi_g[:, 0, :], both)
             k_to_partitions(nc, psum_t, ident[:], wi_rows[4:8], wi_g[:, 1, :], both)
             for chunk in range(ACC_BANKS, CHUNKS):
@@ -230,11 +238,18 @@ def tile_smcrossbaby_1_pb_kernel(
             transpose_block(0)
             transpose_block(1)
             for g in range(Z_PASSES):
-                nc.vector.tensor_tensor(
-                    out=z_g[:, g, :].rearrange("p (n t) -> p n t", t=PACK),
-                    in0=second[:, PACK * g : PACK * (g + 1), :].rearrange("p t n -> p n t"),
-                    in1=inter[:, PACK * g : PACK * (g + 1), :].rearrange("p t n -> p n t"),
-                    op=ADD,
+                for q in range(2 * g, 2 * g + 2):
+                    nc.vector.tensor_tensor(
+                        out=z_rows[:, 2 * q : 2 * q + 2, :],
+                        in0=second[:, 2 * q : 2 * q + 2, :],
+                        in1=inter[:, 2 * q : 2 * q + 2, :],
+                        op=ADD,
+                    )
+                nc.vector.tensor_copy(
+                    out=z_g[:, g, :].rearrange("p (c i t) -> p c t i", i=4, t=PACK),
+                    in_=z_rows[:, PACK * g : PACK * (g + 1), :].rearrange(
+                        "p t (c i) -> p c t i", i=4
+                    ),
                 )
             quantise_block(0)
             quantise(

from contextlib import ExitStack

import concourse.mybir as mybir
from concourse.masks import make_identity

F32 = mybir.dt.float32
BF16 = mybir.dt.bfloat16
U32 = mybir.dt.uint32
U8 = mybir.dt.uint8
FP8X4 = mybir.dt.float8_e4m3fn_x4
RELU = mybir.ActivationFunctionType.Relu
ADD = mybir.AluOpType.add
MULT = mybir.AluOpType.mult

P = 128
PACK = 4
K_PASS = P * PACK
B, E, M, V = 512, 512, 1024, 4096
B_TILES = B // P
CHUNKS = M // P
Z_PASSES = M // K_PASS
V_BLOCK = 512
V_BLOCKS = V // V_BLOCK
V_TILES = V_BLOCK // P
ACC_BANKS = 4

FLOPS = 2 * B * E * M * 2 + 2 * B * M * V


def k_to_partitions(nc, psum_t, ident, pieces, grouped, copies):
    words = grouped.bitcast(F32)
    for i in range(len(pieces) // 2):
        bank = psum_t.tile([P, 2, 2, P], F32, tag="bank")
        for a in range(2):
            piece = pieces[2 * i + a].bitcast(F32)
            for u in range(2):
                nc.tensor.transpose(bank[:, a, u, :], piece[:, u * P : (u + 1) * P], ident)
        copies[i % len(copies)](
            out=words[:, 4 * P * i : 4 * P * (i + 1)].rearrange(
                "p (a c u) -> p a c u", a=2, u=2
            ),
            in_=bank[:].rearrange("p a u c -> p a c u"),
        )


def tile_smcrossbaby_1_pb_kernel(
    tc, y2, first, w_second, b_second, w_int, b_int, w_out, b_out, out
):
    nc = tc.nc
    with ExitStack() as ctx:
        const = ctx.enter_context(tc.tile_pool(name="const", bufs=1))
        raw = ctx.enter_context(tc.tile_pool(name="raw", bufs=8))
        group = ctx.enter_context(tc.tile_pool(name="group", bufs=3))
        keep = ctx.enter_context(tc.tile_pool(name="keep", bufs=1))
        psum_t = ctx.enter_context(tc.psum_pool(name="psum_t", bufs=4))
        psum_acc = ctx.enter_context(tc.psum_pool(name="psum_acc", bufs=ACC_BANKS))
        ctx.enter_context(tc.manual_schedule())

        ident = const.tile([P, P], F32)
        make_identity(nc, ident[:])
        ident_bf = const.tile([P, P], BF16)
        make_identity(nc, ident_bf[:])
        bo_rows = const.tile([P, V_BLOCK], BF16)
        nc.vector.memset(bo_rows[:], 0.0)
        bias_rows = const.tile([P, 2 * P], BF16)
        nc.vector.memset(bias_rows[:], 0.0)

        nc.sync.dma_start(
            out=bo_rows[0:V_BLOCKS, :], in_=b_out.rearrange("(j n) -> j n", j=V_BLOCKS)
        )
        nc.sync.dma_start(out=bias_rows[0:4, :], in_=b_second.rearrange("(q x) -> q x", q=4))
        nc.sync.dma_start(out=bias_rows[4:8, :], in_=b_int.rearrange("(q x) -> q x", q=4))
        y2_raw = raw.tile([P, B_TILES, E], BF16, tag="raw")
        nc.sync.dma_start(out=y2_raw[:], in_=y2.rearrange("(c r) k -> c r k", r=B_TILES))
        w2_raw = raw.tile([P, 4, 2, E], BF16, tag="raw")
        nc.sync.dma_start(
            out=w2_raw[:], in_=w_second.rearrange("(q c e) k -> c q e k", q=4, e=2)
        )
        wi_raw = raw.tile([P, 4, 2, E], BF16, tag="raw")
        nc.sync.dma_start(
            out=wi_raw[:], in_=w_int.rearrange("(q c e) k -> c q e k", q=4, e=2)
        )
        first_raw = raw.tile([P, B_TILES, M], BF16, tag="raw")
        nc.sync.dma_start(
            out=first_raw[:], in_=first.rearrange("(c r) m -> c r m", r=B_TILES)
        )
        wo_raw = []
        for j in range(V_BLOCKS):
            wo_raw.append(raw.tile([P, V_TILES, M], BF16, tag="raw", name="wo_raw%d" % j))
            nc.sync.dma_start(
                out=wo_raw[j][:],
                in_=w_out[j * V_BLOCK : (j + 1) * V_BLOCK, :].rearrange(
                    "(s c) k -> c s k", s=V_TILES
                ),
            )

        both = [nc.scalar.copy, nc.vector.tensor_copy]

        bias_split = const.tile([P, 2, P], F32)
        nc.vector.tensor_copy(
            out=bias_split[:], in_=bias_rows[:].rearrange("p (c e) -> p e c", e=2)
        )
        bias_t = psum_t.tile([P, 2, 2, P], F32, tag="bank")
        for e in range(2):
            nc.tensor.transpose(bias_t[:, 0, e, :], bias_split[:, e, :], ident[:])
        bias = const.tile([P, 2, CHUNKS], F32)
        nc.vector.tensor_copy(
            out=bias[:].rearrange("p w (q e) -> p w q e", e=2),
            in_=bias_t[:, 0, :, 0:8].rearrange("p e (w q) -> p w q e", w=2),
        )

        bo = const.tile([P, V], BF16)

        def spread_b_out(pair):
            spread = psum_acc.tile([P, 2, V_BLOCK], BF16, tag="acc")
            for i in range(2):
                j = 2 * pair + i
                nc.tensor.matmul(
                    out=spread[:, i, :],
                    lhsT=ident_bf[:, j : j + 1].to_broadcast([P, P]),
                    rhs=bo_rows[:],
                    start=True,
                    stop=True,
                )
            nc.scalar.copy(
                out=bo[:, 2 * pair * V_BLOCK : 2 * (pair + 1) * V_BLOCK],
                in_=spread[:].rearrange("p i n -> p (i n)"),
            )

        y2_c = keep.tile([P, B], U32, align_bytes=64)
        y2_s = keep.tile([P, B], U8, align_bytes=64)
        w2_c = keep.tile([P, M], U32, align_bytes=64)
        w2_s = keep.tile([P, M], U8, align_bytes=64)
        wi_c = keep.tile([P, M], U32, align_bytes=64)
        wi_s = keep.tile([P, M], U8, align_bytes=64)

        def quantise(codes, scales, grouped):
            nc.vector.quantize_mx(out=codes.bitcast(FP8X4), scales=scales, in_=grouped)

        y2_g = group.tile([P, B * PACK], BF16, tag="group", align_bytes=64)
        w2_g = group.tile([P, 2, M * PACK // 2], BF16, tag="group", align_bytes=64)
        wi_g = group.tile([P, 2, M * PACK // 2], BF16, tag="group", align_bytes=64)
        w2_rows = [w2_raw[:, q, e, :] for q in range(4) for e in range(2)]
        wi_rows = [wi_raw[:, q, e, :] for q in range(4) for e in range(2)]
        spread_b_out(0)
        spread_b_out(1)
        k_to_partitions(
            nc,
            psum_t,
            ident[:],
            [y2_raw[:, r, :] for r in range(B_TILES)],
            y2_g[:],
            [nc.scalar.copy],
        )
        quantise(y2_c[:], y2_s[:], y2_g[:])
        spread_b_out(2)
        spread_b_out(3)
        k_to_partitions(nc, psum_t, ident[:], w2_rows[0:4], w2_g[:, 0, :], [nc.scalar.copy])
        k_to_partitions(nc, psum_t, ident[:], w2_rows[4:8], w2_g[:, 1, :], [nc.scalar.copy])
        quantise(w2_c[:, 0 : M // 2], w2_s[:, 0 : M // 2], w2_g[:, 0, :])
        quantise(w2_c[:, M // 2 : M], w2_s[:, M // 2 : M], w2_g[:, 1, :])

        z_c = keep.tile([P, Z_PASSES, B], U32, align_bytes=64)
        z_s = keep.tile([P, Z_PASSES, B], U8, align_bytes=64)
        wo_c = keep.tile([P, V_BLOCKS, Z_PASSES, V_BLOCK], U32, align_bytes=64)
        wo_s = keep.tile([P, V_BLOCKS, Z_PASSES, V_BLOCK], U8, align_bytes=64)
        wo_g = [None] * V_BLOCKS

        def transpose_block(j):
            wo_g[j] = group.tile(
                [P, Z_PASSES * V_BLOCK * PACK], BF16, tag="group", align_bytes=64, name="wo_g%d" % j
            )
            k_to_partitions(
                nc,
                psum_t,
                ident[:],
                [
                    wo_raw[j][:, s, g * K_PASS : (g + 1) * K_PASS]
                    for g in range(Z_PASSES)
                    for s in range(V_TILES)
                ],
                wo_g[j][:],
                [nc.scalar.copy],
            )

        def quantise_block(j):
            quantise(
                wo_c[:, j, :, :].rearrange("p g n -> p (g n)"),
                wo_s[:, j, :, :].rearrange("p g n -> p (g n)"),
                wo_g[j][:],
            )

        def hidden_layer(w_c, w_s, chunk, bias_col, result):
            cols = slice(chunk * P, (chunk + 1) * P)
            acc = psum_acc.tile([P, B], F32, tag="acc")
            nc.tensor.matmul_mx(
                out=acc[:],
                lhsT=w_c[:, cols].bitcast(FP8X4),
                lhsT_scale=w_s[:, cols],
                rhs=y2_c[:].bitcast(FP8X4),
                rhs_scale=y2_s[:],
                start=True,
                stop=True,
            )
            nc.scalar.activation(out=result, in_=acc[:], func=RELU, bias=bias_col)

        with tc.tile_pool(name="hidden", bufs=1) as hidden:
            second = hidden.tile([P, CHUNKS, B], F32)
            inter = hidden.tile([P, CHUNKS, B], F32)
            z_rows = hidden.tile([P, CHUNKS, B], BF16)
            z_g = hidden.tile([P, Z_PASSES, B * PACK], BF16, align_bytes=64)
            for chunk in range(ACC_BANKS):
                hidden_layer(w2_c, w2_s, chunk, bias[:, 0, chunk : chunk + 1], second[:, chunk, :])
            k_to_partitions(nc, psum_t, ident[:], wi_rows[0:4], wi_g[:, 0, :], both)
            k_to_partitions(nc, psum_t, ident[:], wi_rows[4:8], wi_g[:, 1, :], both)
            for chunk in range(ACC_BANKS, CHUNKS):
                hidden_layer(w2_c, w2_s, chunk, bias[:, 0, chunk : chunk + 1], second[:, chunk, :])
            quantise(wi_c[:, 0 : M // 2], wi_s[:, 0 : M // 2], wi_g[:, 0, :])
            quantise(wi_c[:, M // 2 : M], wi_s[:, M // 2 : M], wi_g[:, 1, :])
            first_t = []
            for q in range(4):
                first_t.append(psum_t.tile([P, B], F32, tag="bank", name="first_t%d" % q))
                for r in range(B_TILES):
                    nc.tensor.transpose(
                        first_t[q][:, r * P : (r + 1) * P],
                        first_raw[:, r, :].bitcast(F32)[:, q * P : (q + 1) * P],
                        ident[:],
                    )
            for q in range(4):
                nc.vector.tensor_tensor(
                    out=second[:, 2 * q : 2 * q + 2, :],
                    in0=second[:, 2 * q : 2 * q + 2, :],
                    in1=first_t[q][:].bitcast(BF16).rearrange("p (n e) -> p e n", e=2),
                    op=MULT,
                )
            for chunk in range(CHUNKS):
                hidden_layer(wi_c, wi_s, chunk, bias[:, 1, chunk : chunk + 1], inter[:, chunk, :])
            transpose_block(0)
            transpose_block(1)
            for g in range(Z_PASSES):
                for q in range(2 * g, 2 * g + 2):
                    nc.vector.tensor_tensor(
                        out=z_rows[:, 2 * q : 2 * q + 2, :],
                        in0=second[:, 2 * q : 2 * q + 2, :],
                        in1=inter[:, 2 * q : 2 * q + 2, :],
                        op=ADD,
                    )
                nc.vector.tensor_copy(
                    out=z_g[:, g, :].rearrange("p (c i t) -> p c t i", i=4, t=PACK),
                    in_=z_rows[:, PACK * g : PACK * (g + 1), :].rearrange(
                        "p t (c i) -> p c t i", i=4
                    ),
                )
            quantise_block(0)
            quantise(
                z_c[:].rearrange("p g n -> p (g n)"),
                z_s[:].rearrange("p g n -> p (g n)"),
                z_g[:].rearrange("p g x -> p (g x)"),
            )

        out_rows = out.rearrange("(c r) v -> c r v", r=B_TILES)
        with tc.tile_pool(name="result", bufs=2 * B_TILES) as result:
            for j in range(V_BLOCKS):
                if j + 1 < V_BLOCKS:
                    quantise_block(j + 1)
                if j + 2 < V_BLOCKS:
                    transpose_block(j + 2)
                cols = slice(j * V_BLOCK, (j + 1) * V_BLOCK)
                for r in range(B_TILES):
                    rows = slice(r * P, (r + 1) * P)
                    acc = psum_acc.tile([P, V_BLOCK], F32, tag="acc")
                    for g in range(Z_PASSES):
                        nc.tensor.matmul_mx(
                            out=acc[:],
                            lhsT=z_c[:, g, rows].bitcast(FP8X4),
                            lhsT_scale=z_s[:, g, rows],
                            rhs=wo_c[:, j, g, :].bitcast(FP8X4),
                            rhs_scale=wo_s[:, j, g, :],
                            start=(g == 0),
                            stop=(g == Z_PASSES - 1),
                        )
                    res = result.tile([P, V_BLOCK], F32)
                    nc.vector.tensor_tensor(out=res[:], in0=acc[:], in1=bo[:, cols], op=ADD)
                    nc.sync.dma_start(out=out_rows[:, r, cols], in_=res[:])
